import numpy as np
import ml_dtypes


def mxq(x, axis, fmt="e4m3"):
    dtype, down = {"e4m3": (ml_dtypes.float8_e4m3fn, 7), "e5m2": (ml_dtypes.float8_e5m2, 14)}[fmt]
    v = np.moveaxis(np.asarray(x, np.float32).astype(ml_dtypes.bfloat16).astype(np.float64), axis, -1)
    blocks = v.reshape(v.shape[:-1] + (-1, 32))
    amax = np.abs(blocks).max(-1, keepdims=True)
    byte = np.maximum(np.where(amax > 0, np.frexp(amax)[1] - 1 + 127, 0) - down, 1)
    scale = np.exp2(byte - 127.0)
    codes = (blocks / scale).astype(np.float32).astype(dtype).astype(np.float64)
    return np.moveaxis((codes * scale).reshape(v.shape), -1, axis)


WIDE = False


def mx_kscale(k):
    if not WIDE:
        return np.ones(k)
    levels = np.array([10, -10, 5, -5, 0])
    if k % 512:
        return np.exp2(np.random.permutation(np.resize(levels, k // 32))).repeat(32)
    a = np.empty((k // 512, 16))
    for p in range(k // 512):
        a[p, :8] = np.random.permutation(np.resize(levels, 8))
        for g in range(8):
            far = levels[np.abs(levels - a[p, g]) >= 10]
            a[p, g + 8] = far[np.random.randint(len(far))]
    return np.exp2(a.ravel()).repeat(32)


BF16 = ml_dtypes.bfloat16


def bf(x):
    return np.asarray(x, np.float32).astype(BF16)


def f64(x):
    return np.asarray(x).astype(np.float64)


B, T, C, NH, HS, NLQ, NLKV, DHR = 4, 1024, 512, 2, 256, 512, 512, 128
THETA = 10000.0


def rope(v, cos, sin):
    vr = v.reshape(v.shape[:-1] + (-1, 2))
    re, im = vr[..., 0], vr[..., 1]
    c = cos[None, :, None, :]
    s = sin[None, :, None, :]
    return np.stack([re * c - im * s, re * s + im * c], axis=-1).reshape(v.shape)


def setup_inputs():
    s, t = mx_kscale(C), mx_kscale(NLQ)
    ang = np.outer(np.arange(T), 1.0 / THETA ** (np.arange(0, DHR, 2) / DHR))
    return {"x": bf(np.random.standard_normal((B, T, C)) * s),
            "cos": bf(np.cos(ang)),
            "sin": bf(np.sin(ang)),
            "W_dq": bf(np.random.standard_normal((NLQ, C)) / np.sqrt(C) / s[None, :] * t[:, None]),
            "W_uq": bf((np.random.standard_normal((NLQ, C)) / np.sqrt(NLQ) / t[:, None]).reshape(C, NLQ)),
            "W_uk": bf(np.random.standard_normal((C, NLKV)) / np.sqrt(HS)),
            "W_qr": bf(np.random.standard_normal((NH * DHR, NLQ)) / np.sqrt(NLQ) / t[None, :])}


def reference(x, cos, sin, W_dq, W_uq, W_uk, W_qr):
    cq = mxq(mxq(f64(x), 2, "e4m3") @ mxq(f64(W_dq), 1, "e4m3").T, 2, "e4m3")
    k_eff = f64(W_uq).reshape(NLQ, NH, HS).transpose(1, 0, 2) @ f64(W_uk).reshape(NH, HS, NLKV)
    q_abs = cq[:, None] @ mxq(k_eff, 1, "e4m3")[None]
    c_qr = (cq @ mxq(f64(W_qr), 1, "e4m3").T).reshape(B, T, NH, DHR)
    return q_abs, rope(c_qr, f64(cos), f64(sin))

@@ -1,0 +1,262 @@
+from contextlib import ExitStack
+
+import concourse.mybir as mybir
+from concourse.masks import make_identity
+
+F32 = mybir.dt.float32
+BF16 = mybir.dt.bfloat16
+U32 = mybir.dt.uint32
+U8 = mybir.dt.uint8
+FP8X4 = mybir.dt.float8_e4m3fn_x4
+MULT = mybir.AluOpType.mult
+ADD = mybir.AluOpType.add
+
+B, T, C = 4, 1024, 512
+NH, HS = 2, 256
+NLQ, NLKV, DHR = 512, 512, 128
+
+P = 128
+PACK = 4
+WORDS = 2
+ROT = NH * DHR
+TILES_PER_BATCH = T // P
+PAIR = 2
+GROUP = 4
+N_PAIRS = B * TILES_PER_BATCH // PAIR
+N_GROUPS = B * TILES_PER_BATCH // GROUP
+GROUPS_PER_BATCH = TILES_PER_BATCH // GROUP
+
+FLOPS = 2 * B * T * NLQ * (C + NH * NLKV + ROT) + 2 * NH * NLQ * HS * NLKV
+
+
+def quantise(nc, grouped, operand):
+    codes, scales = operand
+    nc.vector.quantize_mx(
+        out=codes.bitcast(FP8X4), scales=scales, in_=grouped.rearrange("p c t -> p (c t)")
+    )
+
+
+def columns(operand, first, count):
+    codes, scales = operand
+    return codes[:, first : first + count], scales[:, first : first + count]
+
+
+def mx_pass(nc, out, stationary, moving):
+    nc.tensor.matmul_mx(
+        out=out,
+        lhsT=stationary[0].bitcast(FP8X4),
+        lhsT_scale=stationary[1],
+        rhs=moving[0].bitcast(FP8X4),
+        rhs_scale=moving[1],
+        start=True,
+        stop=True,
+    )
+
+
+def tile_causalselfattention_pa_t_kernel(tc, x, cos, sin, W_dq, W_uq, W_uk, W_qr, out_0, out_1):
+    nc = tc.nc
+    with ExitStack() as ctx:
+        ctx.enter_context(tc.manual_schedule())
+        const = ctx.enter_context(tc.tile_pool(name="const", bufs=1))
+        grouped_pool = ctx.enter_context(tc.tile_pool(name="grouped", bufs=2))
+        mx_pool = ctx.enter_context(tc.tile_pool(name="mx", bufs=3))
+        rope_pool = ctx.enter_context(tc.tile_pool(name="rope", bufs=3))
+        rows_pool = ctx.enter_context(tc.tile_pool(name="rows", bufs=6))
+        tr_banks = ctx.enter_context(tc.psum_pool(name="tr_banks", bufs=1))
+        cq_banks = ctx.enter_context(tc.psum_pool(name="cq_banks", bufs=2))
+        qa_banks = ctx.enter_context(tc.psum_pool(name="qa_banks", bufs=4))
+        qr_banks = ctx.enter_context(tc.psum_pool(name="qr_banks", bufs=1))
+
+        def mx_tiles(pool, width, name):
+            codes = pool.tile([P, width], U32, name=name + "_codes", tag=name + "_codes", align_bytes=64)
+            scales = pool.tile([P, width], U8, name=name + "_scales", tag=name + "_scales", align_bytes=64)
+            return codes[:], scales[:]
+
+        x_view = x.rearrange("b (p a) k -> b p a k", a=TILES_PER_BATCH)
+        x_words = []
+
+        def load_x(group):
+            b, part = divmod(group, GROUPS_PER_BATCH)
+            x_rows = const.tile([P, GROUP, C], BF16, name="x_rows%d" % group)
+            nc.sync.dma_start(out=x_rows[:], in_=x_view[b, :, part * GROUP : (part + 1) * GROUP, :])
+            x_words.append(x_rows[:].bitcast(F32))
+
+        wuq_rows = const.tile([P, PACK, NH * HS], BF16)
+        nc.sync.dma_start(out=wuq_rows[:], in_=W_uq.rearrange("(m j) c -> m j c", j=PACK))
+        trig = const.tile([P, 3, TILES_PER_BATCH, DHR // 2], BF16)
+        nc.sync.dma_start(out=trig[:, 1, :, :], in_=cos.rearrange("(p a) i -> p a i", a=TILES_PER_BATCH))
+        nc.sync.dma_start(out=trig[:, 2, :, :], in_=sin.rearrange("(p a) i -> p a i", a=TILES_PER_BATCH))
+        wdq_rows = const.tile([P, PACK, C], BF16)
+        nc.sync.dma_start(out=wdq_rows[:], in_=W_dq.rearrange("(m j) k -> m j k", j=PACK))
+        load_x(0)
+        wuk_rows = const.tile([P, NH, WORDS, NLKV], BF16)
+        nc.sync.dma_start(out=wuk_rows[:], in_=W_uk.rearrange("(h q e) n -> q h e n", h=NH, e=WORDS))
+        wqr_rows = const.tile([P, 2, NLQ], BF16)
+        nc.sync.dma_start(out=wqr_rows[:], in_=W_qr.rearrange("(m e) l -> m e l", e=2))
+        for group in range(1, N_GROUPS):
+            load_x(group)
+
+        identity = const.tile([P, P], F32)
+        make_identity(nc, identity[:])
+
+        def times(out, in0, factor):
+            nc.gpsimd.tensor_scalar(out=out, in0=in0, scalar1=factor, scalar2=0.0, op0=MULT, op1=ADD)
+
+        times(trig[:, 0, :, :], trig[:, 2, :, :], -1.0)
+        rotation = const.tile([P, TILES_PER_BATCH, 2, P, 2], F32)
+        for e in range(2):
+            for h in range(NH):
+                times(
+                    rotation[:, :, e, h * (DHR // 2) : (h + 1) * (DHR // 2), :],
+                    trig[:, 1 - e : 3 - e, :, :].rearrange("p f a i -> p a i f"),
+                    1.0,
+                )
+
+        def transpose_two_tiles(bank, tiles_of_words):
+            for s, words in enumerate(tiles_of_words):
+                for u in range(WORDS):
+                    nc.tensor.transpose(bank[:, u, s * P : (s + 1) * P], words[:, u : WORDS * P : WORDS], identity[:])
+
+        def regroup_words(copy, grouped, bank):
+            copy(out=grouped.bitcast(F32), in_=bank[:].rearrange("p u c -> p c u"))
+
+        wuq_words = wuq_rows[:].bitcast(F32)
+        wuq_t = []
+        for h, copy in enumerate((nc.scalar.copy, nc.vector.tensor_copy)):
+            bank = qa_banks.tile([P, PACK, P], F32, tag="bank")
+            for j in range(PACK):
+                nc.tensor.transpose(bank[:, j, :], wuq_words[:, j, h * P : (h + 1) * P], identity[:])
+            transposed = const.tile([P, PACK * P], F32, name="wuq_t%d" % h)
+            copy(out=transposed[:], in_=bank[:].rearrange("p j m -> p (j m)"))
+            wuq_t.append(transposed[:].bitcast(BF16).rearrange("p (c e) -> p c e", e=WORDS))
+
+        wdq_words = wdq_rows[:].bitcast(F32)
+        wdq_grouped = const.tile([P, NLQ, PACK], BF16, align_bytes=64)
+        wdq_mx = mx_tiles(const, NLQ, "wdq")
+        for half, copy in enumerate((nc.scalar.copy, nc.vector.tensor_copy)):
+            bank = qa_banks.tile([P, WORDS, PAIR * P], F32, tag="bank")
+            transpose_two_tiles(bank, [wdq_words[:, PAIR * half + s, :] for s in range(PAIR)])
+            regroup_words(copy, wdq_grouped[:, PAIR * P * half : PAIR * P * (half + 1), :], bank)
+        quantise(nc, wdq_grouped[:], wdq_mx)
+
+        x_mx = {}
+        cq_mx = {}
+        x_grouped = {}
+        cq_grouped = {}
+
+        def transpose_x(pair):
+            group, first = divmod(pair * PAIR, GROUP)
+            bank = tr_banks.tile([P, WORDS, PAIR * P], F32, tag="bank")
+            transpose_two_tiles(bank, [x_words[group][:, first + s, :] for s in range(PAIR)])
+            grouped = grouped_pool.tile([P, PAIR * P, PACK], BF16, tag="x", align_bytes=64)
+            regroup_words(nc.scalar.copy, grouped[:], bank)
+            x_grouped[pair] = grouped
+
+        def quantise_x(pair):
+            x_mx[pair] = mx_tiles(mx_pool, PAIR * P, "x")
+            quantise(nc, x_grouped[pair][:], x_mx[pair])
+
+        def project_cq(pair):
+            grouped = grouped_pool.tile([P, PAIR * P, PACK], BF16, tag="cq", align_bytes=64)
+            for s in range(PAIR):
+                bank = cq_banks.tile([P, PACK, P], F32, tag="bank")
+                for j in range(PACK):
+                    mx_pass(nc, bank[:, j, :], columns(wdq_mx, j * P, P), columns(x_mx[pair], s * P, P))
+                nc.vector.tensor_copy(
+                    out=grouped[:, s * P : (s + 1) * P, :], in_=bank[:].rearrange("p j t -> p t j")
+                )
+            cq_grouped[pair] = grouped
+
+        def quantise_cq(pair):
+            cq_mx[pair] = mx_tiles(mx_pool, PAIR * P, "cq")
+            quantise(nc, cq_grouped[pair][:], cq_mx[pair])
+
+        transpose_x(0)
+        quantise_x(0)
+
+        keff_grouped = const.tile([P, NH * NLKV, PACK], BF16, align_bytes=64)
+        keff_mx = mx_tiles(const, NH * NLKV, "keff")
+
+        def make_keff(h):
+            for n_block in range(NLKV // P):
+                bank = qa_banks.tile([P, PACK, P], F32, tag="bank")
+                for j in range(PACK):
+                    for e in range(WORDS):
+                        nc.tensor.matmul(
+                            out=bank[:, j, :],
+                            lhsT=wuq_t[h][:, j * P : (j + 1) * P, e],
+                            rhs=wuk_rows[:, h, e, n_block * P : (n_block + 1) * P],
+                            start=(e == 0),
+                            stop=(e == WORDS - 1),
+                        )
+                copy = nc.scalar.copy if n_block % 2 == 0 else nc.vector.tensor_copy
+                first = h * NLKV + n_block * P
+                copy(out=keff_grouped[:, first : first + P, :], in_=bank[:].rearrange("p j n -> p n j"))
+            quantise(nc, keff_grouped[:, h * NLKV : (h + 1) * NLKV, :], columns(keff_mx, h * NLKV, NLKV))
+
+        make_keff(0)
+        project_cq(0)
+        transpose_x(1)
+
+        wqr_words = wqr_rows[:].bitcast(F32).rearrange("m e (p u) -> m e u p", u=WORDS)
+        wqr_grouped = const.tile([P, ROT, PACK], BF16, align_bytes=64)
+        wqr_mx = mx_tiles(const, ROT, "wqr")
+        bank = qr_banks.tile([P, WORDS, ROT], F32, tag="bank")
+        for e in range(2):
+            for u in range(WORDS):
+                nc.tensor.transpose(bank[:, u, e * P : (e + 1) * P], wqr_words[:, e, u, :], identity[:])
+        regroup_words(nc.scalar.copy, wqr_grouped[:], bank)
+        quantise_cq(0)
+        quantise_x(1)
+        quantise(nc, wqr_grouped[:], wqr_mx)
+
+        make_keff(1)
+
+        q_abs_view = out_0.rearrange("b h (p a) n -> b h p a n", a=TILES_PER_BATCH)
+        q_r_view = out_1.rearrange("b (p a) h d -> b p a (h d)", a=TILES_PER_BATCH)
+        for pair in range(N_PAIRS):
+            b, a = divmod(pair * PAIR, TILES_PER_BATCH)
+            last = pair == N_PAIRS - 1
+
+            if pair + 2 < N_PAIRS:
+                transpose_x(pair + 2)
+            if pair + 1 < N_PAIRS:
+                project_cq(pair + 1)
+
+            rot_bank = qr_banks.tile([P, PAIR, 2 * P], F32, tag="bank")
+            for s in range(PAIR):
+                mx_pass(nc, rot_bank[:, s, :], columns(cq_mx[pair], s * P, P), wqr_mx)
+
+            products = rope_pool.tile([P, PAIR, 2, P, 2], F32, tag="products")
+
+            def rotate(s):
+                nc.vector.tensor_tensor(
+                    out=products[:, s, :, :, :].rearrange("p e m f -> p (e m) f"),
+                    in0=rot_bank[:, s, :].unsqueeze(2).to_broadcast([P, 2 * P, 2]),
+                    in1=rotation[:, a + s, :, :, :].rearrange("p e m f -> p (e m) f"),
+                    op=MULT,
+                )
+
+            rotate(0)
+            if pair + 2 < N_PAIRS:
+                quantise_x(pair + 2)
+            if pair + 1 < N_PAIRS:
+                quantise_cq(pair + 1)
+            rotate(1)
+            q_r_rows = rows_pool.tile([P, PAIR, ROT], F32, tag="q_r")
+            nc.gpsimd.tensor_tensor(
+                out=q_r_rows[:],
+                in0=products[:, :, 0, :, :].rearrange("p s m f -> p s (m f)"),
+                in1=products[:, :, 1, :, :].rearrange("p s m f -> p s (m f)"),
+                op=ADD,
+            )
+
+            for h in range(NH):
+                q_abs_rows = rows_pool.tile([P, PAIR, NLKV], F32, tag="q_abs")
+                for s in range(PAIR):
+                    acc = qa_banks.tile([P, NLKV], F32, tag="bank")
+                    mx_pass(nc, acc[:], columns(cq_mx[pair], s * P, P), columns(keff_mx, h * NLKV, NLKV))
+                    copy = nc.vector.tensor_copy if last and s == 1 else nc.scalar.copy
+                    copy(out=q_abs_rows[:, s, :], in_=acc[:])
+                nc.sync.dma_start(out=q_abs_view[b, h, :, a : a + PAIR, :], in_=q_abs_rows[:])
+            nc.sync.dma_start(out=q_r_view[b, :, a : a + PAIR, :], in_=q_r_rows[:])

@@ -58,10 +58,10 @@ def tile_causalselfattention_pa_t_kernel(tc, x, cos, sin, W_dq, W_uq, W_uk, W_qr
     with ExitStack() as ctx:
         ctx.enter_context(tc.manual_schedule())
         const = ctx.enter_context(tc.tile_pool(name="const", bufs=1))
-        grouped_pool = ctx.enter_context(tc.tile_pool(name="grouped", bufs=2))
-        mx_pool = ctx.enter_context(tc.tile_pool(name="mx", bufs=3))
+        grouped_pool = ctx.enter_context(tc.tile_pool(name="grouped", bufs=3))
+        mx_pool = ctx.enter_context(tc.tile_pool(name="mx", bufs=4))
         rope_pool = ctx.enter_context(tc.tile_pool(name="rope", bufs=3))
-        rows_pool = ctx.enter_context(tc.tile_pool(name="rows", bufs=6))
+        rows_pool = ctx.enter_context(tc.tile_pool(name="rows", bufs=8))
         tr_banks = ctx.enter_context(tc.psum_pool(name="tr_banks", bufs=1))
         cq_banks = ctx.enter_context(tc.psum_pool(name="cq_banks", bufs=2))
         qa_banks = ctx.enter_context(tc.psum_pool(name="qa_banks", bufs=4))
@@ -75,42 +75,48 @@ def tile_causalselfattention_pa_t_kernel(tc, x, cos, sin, W_dq, W_uq, W_uk, W_qr
         x_view = x.rearrange("b (p a) k -> b p a k", a=TILES_PER_BATCH)
         x_words = []
 
-        def load_x(group):
-            b, part = divmod(group, GROUPS_PER_BATCH)
-            x_rows = const.tile([P, GROUP, C], BF16, name="x_rows%d" % group)
-            nc.sync.dma_start(out=x_rows[:], in_=x_view[b, :, part * GROUP : (part + 1) * GROUP, :])
-            x_words.append(x_rows[:].bitcast(F32))
+        def load_x(b, first, count):
+            x_rows = const.tile([P, count, C], BF16, name="x_rows%d" % len(x_words))
+            nc.sync.dma_start(out=x_rows[:], in_=x_view[b, :, first : first + count, :])
+            words = x_rows[:].bitcast(F32)
+            x_words.extend(words[:, s, :] for s in range(count))
 
-        wuq_rows = const.tile([P, PACK, NH * HS], BF16)
-        nc.sync.dma_start(out=wuq_rows[:], in_=W_uq.rearrange("(m j) c -> m j c", j=PACK))
-        trig = const.tile([P, 3, TILES_PER_BATCH, DHR // 2], BF16)
-        nc.sync.dma_start(out=trig[:, 1, :, :], in_=cos.rearrange("(p a) i -> p a i", a=TILES_PER_BATCH))
-        nc.sync.dma_start(out=trig[:, 2, :, :], in_=sin.rearrange("(p a) i -> p a i", a=TILES_PER_BATCH))
-        wdq_rows = const.tile([P, PACK, C], BF16)
-        nc.sync.dma_start(out=wdq_rows[:], in_=W_dq.rearrange("(m j) k -> m j k", j=PACK))
-        load_x(0)
-        wuk_rows = const.tile([P, NH, WORDS, NLKV], BF16)
-        nc.sync.dma_start(out=wuk_rows[:], in_=W_uk.rearrange("(h q e) n -> q h e n", h=NH, e=WORDS))
+        wuq_view = W_uq.rearrange("(m j) c -> m j c", j=PACK)
+        wdq_view = W_dq.rearrange("(m j) k -> m j k", j=PACK)
+
+        def load_halves(view, width, name):
+            halves = []
+            for half in range(2):
+                rows = const.tile([P, 2, width], BF16, name="%s_rows%d" % (name, half))
+                nc.sync.dma_start(out=rows[:], in_=view[:, 2 * half : 2 * half + 2, :])
+                halves.append(rows[:].bitcast(F32))
+            return [halves[j // 2][:, j % 2, :] for j in range(PACK)]
+
+        wuq_words = load_halves(wuq_view, NH * HS, "wuq")
+        wdq_words = load_halves(wdq_view, C, "wdq")
+        load_x(0, 0, PAIR)
+        wuk_view = W_uk.rearrange("(h q e) n -> h q e n", h=NH, e=WORDS)
+        wuk_rows = []
+
+        def load_wuk(h):
+            rows = const.tile([P, WORDS, NLKV], BF16, name="wuk_rows%d" % h)
+            nc.sync.dma_start(out=rows[:], in_=wuk_view[h])
+            wuk_rows.append(rows)
+
+        load_wuk(0)
+        load_x(0, PAIR, PAIR)
+        load_wuk(1)
         wqr_rows = const.tile([P, 2, NLQ], BF16)
         nc.sync.dma_start(out=wqr_rows[:], in_=W_qr.rearrange("(m e) l -> m e l", e=2))
+        trig_rows = const.tile([P, 2, TILES_PER_BATCH, DHR // 2], BF16)
+        for f, table in enumerate((cos, sin)):
+            nc.sync.dma_start(out=trig_rows[:, f, :, :], in_=table.rearrange("(p a) i -> p a i", a=TILES_PER_BATCH))
         for group in range(1, N_GROUPS):
-            load_x(group)
+            b, part = divmod(group, GROUPS_PER_BATCH)
+            load_x(b, part * GROUP, GROUP)
 
         identity = const.tile([P, P], F32)
         make_identity(nc, identity[:])
-
-        def times(out, in0, factor):
-            nc.gpsimd.tensor_scalar(out=out, in0=in0, scalar1=factor, scalar2=0.0, op0=MULT, op1=ADD)
-
-        times(trig[:, 0, :, :], trig[:, 2, :, :], -1.0)
-        rotation = const.tile([P, TILES_PER_BATCH, 2, P, 2], F32)
-        for e in range(2):
-            for h in range(NH):
-                times(
-                    rotation[:, :, e, h * (DHR // 2) : (h + 1) * (DHR // 2), :],
-                    trig[:, 1 - e : 3 - e, :, :].rearrange("p f a i -> p a i f"),
-                    1.0,
-                )
 
         def transpose_two_tiles(bank, tiles_of_words):
             for s, words in enumerate(tiles_of_words):
@@ -120,22 +126,20 @@ def tile_causalselfattention_pa_t_kernel(tc, x, cos, sin, W_dq, W_uq, W_uk, W_qr
         def regroup_words(copy, grouped, bank):
             copy(out=grouped.bitcast(F32), in_=bank[:].rearrange("p u c -> p c u"))
 
-        wuq_words = wuq_rows[:].bitcast(F32)
         wuq_t = []
         for h, copy in enumerate((nc.scalar.copy, nc.vector.tensor_copy)):
             bank = qa_banks.tile([P, PACK, P], F32, tag="bank")
             for j in range(PACK):
-                nc.tensor.transpose(bank[:, j, :], wuq_words[:, j, h * P : (h + 1) * P], identity[:])
+                nc.tensor.transpose(bank[:, j, :], wuq_words[j][:, h * P : (h + 1) * P], identity[:])
             transposed = const.tile([P, PACK * P], F32, name="wuq_t%d" % h)
             copy(out=transposed[:], in_=bank[:].rearrange("p j m -> p (j m)"))
             wuq_t.append(transposed[:].bitcast(BF16).rearrange("p (c e) -> p c e", e=WORDS))
 
-        wdq_words = wdq_rows[:].bitcast(F32)
         wdq_grouped = const.tile([P, NLQ, PACK], BF16, align_bytes=64)
         wdq_mx = mx_tiles(const, NLQ, "wdq")
         for half, copy in enumerate((nc.scalar.copy, nc.vector.tensor_copy)):
             bank = qa_banks.tile([P, WORDS, PAIR * P], F32, tag="bank")
-            transpose_two_tiles(bank, [wdq_words[:, PAIR * half + s, :] for s in range(PAIR)])
+            transpose_two_tiles(bank, wdq_words[PAIR * half : PAIR * (half + 1)])
             regroup_words(copy, wdq_grouped[:, PAIR * P * half : PAIR * P * (half + 1), :], bank)
         quantise(nc, wdq_grouped[:], wdq_mx)
 
@@ -144,119 +148,164 @@ def tile_causalselfattention_pa_t_kernel(tc, x, cos, sin, W_dq, W_uq, W_uk, W_qr
         x_grouped = {}
         cq_grouped = {}
 
+        x_banks = {}
+
         def transpose_x(pair):
-            group, first = divmod(pair * PAIR, GROUP)
-            bank = tr_banks.tile([P, WORDS, PAIR * P], F32, tag="bank")
-            transpose_two_tiles(bank, [x_words[group][:, first + s, :] for s in range(PAIR)])
-            grouped = grouped_pool.tile([P, PAIR * P, PACK], BF16, tag="x", align_bytes=64)
-            regroup_words(nc.scalar.copy, grouped[:], bank)
-            x_grouped[pair] = grouped
+            x_banks[pair] = tr_banks.tile([P, WORDS, PAIR * P], F32, tag="bank", name="bank")
+            transpose_two_tiles(x_banks[pair], x_words[pair * PAIR : (pair + 1) * PAIR])
+
+        def regroup_x(pair):
+            x_grouped[pair] = grouped_pool.tile([P, PAIR * P, PACK], BF16, tag="x", name="x", align_bytes=64)
+            regroup_words(nc.scalar.copy, x_grouped[pair][:], x_banks[pair])
 
         def quantise_x(pair):
             x_mx[pair] = mx_tiles(mx_pool, PAIR * P, "x")
             quantise(nc, x_grouped[pair][:], x_mx[pair])
 
-        def project_cq(pair):
+        def project_cq(pair, copies):
             grouped = grouped_pool.tile([P, PAIR * P, PACK], BF16, tag="cq", align_bytes=64)
             for s in range(PAIR):
                 bank = cq_banks.tile([P, PACK, P], F32, tag="bank")
                 for j in range(PACK):
                     mx_pass(nc, bank[:, j, :], columns(wdq_mx, j * P, P), columns(x_mx[pair], s * P, P))
-                nc.vector.tensor_copy(
-                    out=grouped[:, s * P : (s + 1) * P, :], in_=bank[:].rearrange("p j t -> p t j")
-                )
+                copies[s](out=grouped[:, s * P : (s + 1) * P, :], in_=bank[:].rearrange("p j t -> p t j"))
             cq_grouped[pair] = grouped
 
         def quantise_cq(pair):
             cq_mx[pair] = mx_tiles(mx_pool, PAIR * P, "cq")
             quantise(nc, cq_grouped[pair][:], cq_mx[pair])
 
-        transpose_x(0)
-        quantise_x(0)
-
         keff_grouped = const.tile([P, NH * NLKV, PACK], BF16, align_bytes=64)
         keff_mx = mx_tiles(const, NH * NLKV, "keff")
 
-        def make_keff(h):
-            for n_block in range(NLKV // P):
-                bank = qa_banks.tile([P, PACK, P], F32, tag="bank")
-                for j in range(PACK):
-                    for e in range(WORDS):
-                        nc.tensor.matmul(
-                            out=bank[:, j, :],
-                            lhsT=wuq_t[h][:, j * P : (j + 1) * P, e],
-                            rhs=wuk_rows[:, h, e, n_block * P : (n_block + 1) * P],
-                            start=(e == 0),
-                            stop=(e == WORDS - 1),
-                        )
-                copy = nc.scalar.copy if n_block % 2 == 0 else nc.vector.tensor_copy
-                first = h * NLKV + n_block * P
-                copy(out=keff_grouped[:, first : first + P, :], in_=bank[:].rearrange("p j n -> p n j"))
+        def make_keff(h, n_block, copy):
+            bank = qa_banks.tile([P, PACK, P], F32, tag="bank")
+            for j in range(PACK):
+                for e in range(WORDS):
+                    nc.tensor.matmul(
+                        out=bank[:, j, :],
+                        lhsT=wuq_t[h][:, j * P : (j + 1) * P, e],
+                        rhs=wuk_rows[h][:, e, n_block * P : (n_block + 1) * P],
+                        start=(e == 0),
+                        stop=(e == WORDS - 1),
+                    )
+            first = h * NLKV + n_block * P
+            copy(out=keff_grouped[:, first : first + P, :], in_=bank[:].rearrange("p j n -> p n j"))
+
+        def quantise_keff(h):
             quantise(nc, keff_grouped[:, h * NLKV : (h + 1) * NLKV, :], columns(keff_mx, h * NLKV, NLKV))
 
-        make_keff(0)
-        project_cq(0)
-        transpose_x(1)
-
-        wqr_words = wqr_rows[:].bitcast(F32).rearrange("m e (p u) -> m e u p", u=WORDS)
         wqr_grouped = const.tile([P, ROT, PACK], BF16, align_bytes=64)
         wqr_mx = mx_tiles(const, ROT, "wqr")
-        bank = qr_banks.tile([P, WORDS, ROT], F32, tag="bank")
-        for e in range(2):
-            for u in range(WORDS):
-                nc.tensor.transpose(bank[:, u, e * P : (e + 1) * P], wqr_words[:, e, u, :], identity[:])
-        regroup_words(nc.scalar.copy, wqr_grouped[:], bank)
-        quantise_cq(0)
-        quantise_x(1)
-        quantise(nc, wqr_grouped[:], wqr_mx)
 
-        make_keff(1)
+        def transpose_wqr():
+            wqr_words = wqr_rows[:].bitcast(F32).rearrange("m e (p u) -> m e u p", u=WORDS)
+            bank = qr_banks.tile([P, WORDS, ROT], F32, tag="bank")
+            for e in range(2):
+                for u in range(WORDS):
+                    nc.tensor.transpose(bank[:, u, e * P : (e + 1) * P], wqr_words[:, e, u, :], identity[:])
+            regroup_words(nc.scalar.copy, wqr_grouped[:], bank)
 
         q_abs_view = out_0.rearrange("b h (p a) n -> b h p a n", a=TILES_PER_BATCH)
         q_r_view = out_1.rearrange("b (p a) h d -> b p a (h d)", a=TILES_PER_BATCH)
-        for pair in range(N_PAIRS):
-            b, a = divmod(pair * PAIR, TILES_PER_BATCH)
-            last = pair == N_PAIRS - 1
+        rot_banks = {}
+        products = {}
+        q_r = {}
 
-            if pair + 2 < N_PAIRS:
-                transpose_x(pair + 2)
-            if pair + 1 < N_PAIRS:
-                project_cq(pair + 1)
-
+        def project_cqr(pair):
             rot_bank = qr_banks.tile([P, PAIR, 2 * P], F32, tag="bank")
             for s in range(PAIR):
                 mx_pass(nc, rot_bank[:, s, :], columns(cq_mx[pair], s * P, P), wqr_mx)
+            rot_banks[pair] = rot_bank
+            products[pair] = rope_pool.tile([P, PAIR, 2, P, 2], F32, tag="products", name="products")
 
-            products = rope_pool.tile([P, PAIR, 2, P, 2], F32, tag="products")
+        trig = const.tile([P, TILES_PER_BATCH, 2, 2, DHR // 2], BF16)
 
-            def rotate(s):
+        def make_trig():
+            for e in range(2):
+                nc.scalar.copy(out=trig[:, :, e, e, :], in_=trig_rows[:, 0, :, :])
+            nc.scalar.copy(out=trig[:, :, 0, 1, :], in_=trig_rows[:, 1, :, :])
+            nc.scalar.mul(trig[:, :, 1, 0, :], trig_rows[:, 1, :, :], -1.0)
+
+        def rotate(pair):
+            a = pair * PAIR % TILES_PER_BATCH
+            half = DHR // 2
+            for h in range(NH):
+                heads = slice(h * half, (h + 1) * half)
                 nc.vector.tensor_tensor(
-                    out=products[:, s, :, :, :].rearrange("p e m f -> p (e m) f"),
-                    in0=rot_bank[:, s, :].unsqueeze(2).to_broadcast([P, 2 * P, 2]),
-                    in1=rotation[:, a + s, :, :, :].rearrange("p e m f -> p (e m) f"),
+                    out=products[pair][:, :, :, heads, :].rearrange("p s e i f -> p (s e) i f"),
+                    in0=rot_banks[pair][:].rearrange("p s (e m) -> p (s e) m", e=2)[:, :, heads]
+                    .unsqueeze(3)
+                    .to_broadcast([P, PAIR * 2, half, 2]),
+                    in1=trig[:, a : a + PAIR, :, :, :].rearrange("p s e f i -> p (s e) i f"),
                     op=MULT,
                 )
 
-            rotate(0)
-            if pair + 2 < N_PAIRS:
-                quantise_x(pair + 2)
-            if pair + 1 < N_PAIRS:
-                quantise_cq(pair + 1)
-            rotate(1)
+        def sum_q_r(pair):
+            b, a = divmod(pair * PAIR, TILES_PER_BATCH)
             q_r_rows = rows_pool.tile([P, PAIR, ROT], F32, tag="q_r")
             nc.gpsimd.tensor_tensor(
                 out=q_r_rows[:],
-                in0=products[:, :, 0, :, :].rearrange("p s m f -> p s (m f)"),
-                in1=products[:, :, 1, :, :].rearrange("p s m f -> p s (m f)"),
+                in0=products[pair][:, :, 0, :, :].rearrange("p s m f -> p s (m f)"),
+                in1=products[pair][:, :, 1, :, :].rearrange("p s m f -> p s (m f)"),
                 op=ADD,
             )
+            q_r[pair] = q_r_rows
 
-            for h in range(NH):
-                q_abs_rows = rows_pool.tile([P, PAIR, NLKV], F32, tag="q_abs")
-                for s in range(PAIR):
-                    acc = qa_banks.tile([P, NLKV], F32, tag="bank")
-                    mx_pass(nc, acc[:], columns(cq_mx[pair], s * P, P), columns(keff_mx, h * NLKV, NLKV))
-                    copy = nc.vector.tensor_copy if last and s == 1 else nc.scalar.copy
-                    copy(out=q_abs_rows[:, s, :], in_=acc[:])
-                nc.sync.dma_start(out=q_abs_view[b, h, :, a : a + PAIR, :], in_=q_abs_rows[:])
-            nc.sync.dma_start(out=q_r_view[b, :, a : a + PAIR, :], in_=q_r_rows[:])
+        def store_q_r(pair):
+            b, a = divmod(pair * PAIR, TILES_PER_BATCH)
+            nc.sync.dma_start(out=q_r_view[b, :, a : a + PAIR, :], in_=q_r[pair][:])
+
+        def project_q_abs(pair, h, copies):
+            b, a = divmod(pair * PAIR, TILES_PER_BATCH)
+            q_abs_rows = rows_pool.tile([P, PAIR, NLKV], F32, tag="q_abs")
+            for s in range(PAIR):
+                acc = qa_banks.tile([P, NLKV], F32, tag="bank")
+                mx_pass(nc, acc[:], columns(cq_mx[pair], s * P, P), columns(keff_mx, h * NLKV, NLKV))
+                copies[s](out=q_abs_rows[:, s, :], in_=acc[:])
+            nc.sync.dma_start(out=q_abs_view[b, h, :, a : a + PAIR, :], in_=q_abs_rows[:])
+
+        on_scalar = (nc.scalar.copy, nc.scalar.copy)
+        on_both = (nc.scalar.copy, nc.vector.tensor_copy)
+
+        on_vector = (nc.vector.tensor_copy, nc.vector.tensor_copy)
+
+        transpose_x(0)
+        regroup_x(0)
+        quantise_x(0)
+        make_keff(0, 0, nc.scalar.copy)
+        make_keff(0, 1, nc.vector.tensor_copy)
+        project_cq(0, (nc.vector.tensor_copy, nc.scalar.copy))
+        make_keff(0, 2, nc.scalar.copy)
+        make_keff(0, 3, nc.vector.tensor_copy)
+        transpose_x(1)
+        regroup_x(1)
+        quantise_cq(0)
+        quantise_keff(0)
+        transpose_wqr()
+        quantise_x(1)
+        quantise(nc, wqr_grouped[:], wqr_mx)
+        make_keff(1, 0, nc.scalar.copy)
+        make_keff(1, 1, nc.vector.tensor_copy)
+        make_trig()
+        make_keff(1, 2, nc.scalar.copy)
+        make_keff(1, 3, nc.vector.tensor_copy)
+        quantise_keff(1)
+
+        for pair in range(N_PAIRS):
+            last = pair == N_PAIRS - 1
+            if pair + 2 < N_PAIRS:
+                transpose_x(pair + 2)
+                regroup_x(pair + 2)
+            if not last:
+                project_cq(pair + 1, on_vector)
+            project_q_abs(pair, 0, on_both if last else on_scalar)
+            if pair + 2 < N_PAIRS:
+                quantise_x(pair + 2)
+            project_cqr(pair)
+            rotate(pair)
+            sum_q_r(pair)
+            if not last:
+                quantise_cq(pair + 1)
+            project_q_abs(pair, 1, on_both if last else on_scalar)
+            store_q_r(pair)

@@ -59,7 +59,7 @@ def tile_causalselfattention_pa_t_kernel(tc, x, cos, sin, W_dq, W_uq, W_uk, W_qr
         ctx.enter_context(tc.manual_schedule())
         const = ctx.enter_context(tc.tile_pool(name="const", bufs=1))
         grouped_pool = ctx.enter_context(tc.tile_pool(name="grouped", bufs=3))
-        mx_pool = ctx.enter_context(tc.tile_pool(name="mx", bufs=4))
+        mx_pool = ctx.enter_context(tc.tile_pool(name="mx", bufs=5))
         rope_pool = ctx.enter_context(tc.tile_pool(name="rope", bufs=3))
         rows_pool = ctx.enter_context(tc.tile_pool(name="rows", bufs=8))
         tr_banks = ctx.enter_context(tc.psum_pool(name="tr_banks", bufs=1))
@@ -276,36 +276,39 @@ def tile_causalselfattention_pa_t_kernel(tc, x, cos, sin, W_dq, W_uq, W_uk, W_qr
         make_keff(0, 0, nc.scalar.copy)
         make_keff(0, 1, nc.vector.tensor_copy)
         project_cq(0, (nc.vector.tensor_copy, nc.scalar.copy))
-        make_keff(0, 2, nc.scalar.copy)
-        make_keff(0, 3, nc.vector.tensor_copy)
         transpose_x(1)
         regroup_x(1)
+        make_keff(0, 2, nc.scalar.copy)
+        make_keff(0, 3, nc.vector.tensor_copy)
         quantise_cq(0)
-        quantise_keff(0)
-        transpose_wqr()
         quantise_x(1)
-        quantise(nc, wqr_grouped[:], wqr_mx)
+        transpose_wqr()
         make_keff(1, 0, nc.scalar.copy)
         make_keff(1, 1, nc.vector.tensor_copy)
-        make_trig()
+        quantise_keff(0)
+        transpose_x(2)
+        regroup_x(2)
+        quantise(nc, wqr_grouped[:], wqr_mx)
         make_keff(1, 2, nc.scalar.copy)
         make_keff(1, 3, nc.vector.tensor_copy)
+        quantise_x(2)
+        make_trig()
         quantise_keff(1)
 
         for pair in range(N_PAIRS):
             last = pair == N_PAIRS - 1
-            if pair + 2 < N_PAIRS:
-                transpose_x(pair + 2)
-                regroup_x(pair + 2)
+            if pair + 3 < N_PAIRS:
+                transpose_x(pair + 3)
+                regroup_x(pair + 3)
             if not last:
                 project_cq(pair + 1, on_vector)
-            project_q_abs(pair, 0, on_both if last else on_scalar)
-            if pair + 2 < N_PAIRS:
-                quantise_x(pair + 2)
             project_cqr(pair)
             rotate(pair)
             sum_q_r(pair)
             if not last:
                 quantise_cq(pair + 1)
-            project_q_abs(pair, 1, on_both if last else on_scalar)
+            if pair + 3 < N_PAIRS:
+                quantise_x(pair + 3)
+            for h in range(NH):
+                project_q_abs(pair, h, on_both if last else on_scalar)
             store_q_r(pair)

@@ -92,9 +92,6 @@ def tile_causalselfattention_pa_t_kernel(tc, x, cos, sin, W_dq, W_uq, W_uk, W_qr
                 halves.append(rows[:].bitcast(F32))
             return [halves[j // 2][:, j % 2, :] for j in range(PACK)]
 
-        wuq_words = load_halves(wuq_view, NH * HS, "wuq")
-        wdq_words = load_halves(wdq_view, C, "wdq")
-        load_x(0, 0, PAIR)
         wuk_view = W_uk.rearrange("(h q e) n -> h q e n", h=NH, e=WORDS)
         wuk_rows = []
 
@@ -103,20 +100,37 @@ def tile_causalselfattention_pa_t_kernel(tc, x, cos, sin, W_dq, W_uq, W_uk, W_qr
             nc.sync.dma_start(out=rows[:], in_=wuk_view[h])
             wuk_rows.append(rows)
 
+        wuq_words = load_halves(wuq_view, NH * HS, "wuq")
         load_wuk(0)
+        wdq_words = load_halves(wdq_view, C, "wdq")
+        load_x(0, 0, PAIR)
         load_x(0, PAIR, PAIR)
         load_wuk(1)
         wqr_rows = const.tile([P, 2, NLQ], BF16)
         nc.sync.dma_start(out=wqr_rows[:], in_=W_qr.rearrange("(m e) l -> m e l", e=2))
-        trig_rows = const.tile([P, 2, TILES_PER_BATCH, DHR // 2], BF16)
-        for f, table in enumerate((cos, sin)):
-            nc.sync.dma_start(out=trig_rows[:, f, :, :], in_=table.rearrange("(p a) i -> p a i", a=TILES_PER_BATCH))
-        for group in range(1, N_GROUPS):
+        def load_group(group):
             b, part = divmod(group, GROUPS_PER_BATCH)
             load_x(b, part * GROUP, GROUP)
 
+        load_group(1)
+        trig_rows = const.tile([P, 2, TILES_PER_BATCH, DHR // 2], BF16)
+        for f, table in enumerate((cos, sin)):
+            nc.sync.dma_start(out=trig_rows[:, f, :, :], in_=table.rearrange("(p a) i -> p a i", a=TILES_PER_BATCH))
+        for group in range(2, N_GROUPS):
+            load_group(group)
+
         identity = const.tile([P, P], F32)
         make_identity(nc, identity[:])
+
+        zeros = const.tile([P, NLKV], BF16)
+        nc.vector.memset(zeros[:], 0.0)
+
+        def warm_up(count):
+            for i in range(count):
+                bank = cq_banks.tile([P, NLKV], F32, tag="bank", name="bank")
+                nc.tensor.matmul(out=bank[:], lhsT=zeros[:, 0:P], rhs=zeros[:], start=True, stop=True)
+
+        warm_up(5)
 
         def transpose_two_tiles(bank, tiles_of_words):
             for s, words in enumerate(tiles_of_words):
@@ -134,6 +148,7 @@ def tile_causalselfattention_pa_t_kernel(tc, x, cos, sin, W_dq, W_uq, W_uk, W_qr
             transposed = const.tile([P, PACK * P], F32, name="wuq_t%d" % h)
             copy(out=transposed[:], in_=bank[:].rearrange("p j m -> p (j m)"))
             wuq_t.append(transposed[:].bitcast(BF16).rearrange("p (c e) -> p c e", e=WORDS))
+        warm_up(2)
 
         wdq_grouped = const.tile([P, NLQ, PACK], BF16, align_bytes=64)
         wdq_mx = mx_tiles(const, NLQ, "wdq")
@@ -141,7 +156,6 @@ def tile_causalselfattention_pa_t_kernel(tc, x, cos, sin, W_dq, W_uq, W_uk, W_qr
             bank = qa_banks.tile([P, WORDS, PAIR * P], F32, tag="bank")
             transpose_two_tiles(bank, wdq_words[PAIR * half : PAIR * (half + 1)])
             regroup_words(copy, wdq_grouped[:, PAIR * P * half : PAIR * P * (half + 1), :], bank)
-        quantise(nc, wdq_grouped[:], wdq_mx)
 
         x_mx = {}
         cq_mx = {}
@@ -222,10 +236,10 @@ def tile_causalselfattention_pa_t_kernel(tc, x, cos, sin, W_dq, W_uq, W_uk, W_qr
         trig = const.tile([P, TILES_PER_BATCH, 2, 2, DHR // 2], BF16)
 
         def make_trig():
-            for e in range(2):
-                nc.scalar.copy(out=trig[:, :, e, e, :], in_=trig_rows[:, 0, :, :])
-            nc.scalar.copy(out=trig[:, :, 0, 1, :], in_=trig_rows[:, 1, :, :])
-            nc.scalar.mul(trig[:, :, 1, 0, :], trig_rows[:, 1, :, :], -1.0)
+            for e, f, table, factor in ((0, 0, 0, 1.0), (1, 1, 0, 1.0), (0, 1, 1, 1.0), (1, 0, 1, -1.0)):
+                nc.gpsimd.tensor_scalar(
+                    out=trig[:, :, e, f, :], in0=trig_rows[:, table, :, :], scalar1=factor, scalar2=0.0, op0=MULT, op1=ADD
+                )
 
         def rotate(pair):
             a = pair * PAIR % TILES_PER_BATCH
@@ -270,16 +284,17 @@ def tile_causalselfattention_pa_t_kernel(tc, x, cos, sin, W_dq, W_uq, W_uk, W_qr
 
         on_vector = (nc.vector.tensor_copy, nc.vector.tensor_copy)
 
+        make_keff(0, 0, nc.scalar.copy)
         transpose_x(0)
         regroup_x(0)
+        quantise(nc, wdq_grouped[:], wdq_mx)
         quantise_x(0)
-        make_keff(0, 0, nc.scalar.copy)
         make_keff(0, 1, nc.vector.tensor_copy)
+        make_keff(0, 2, nc.scalar.copy)
+        make_keff(0, 3, nc.vector.tensor_copy)
         project_cq(0, (nc.vector.tensor_copy, nc.scalar.copy))
         transpose_x(1)
         regroup_x(1)
-        make_keff(0, 2, nc.scalar.copy)
-        make_keff(0, 3, nc.vector.tensor_copy)
         quantise_cq(0)
         quantise_x(1)
         transpose_wqr()
@@ -290,7 +305,7 @@ def tile_causalselfattention_pa_t_kernel(tc, x, cos, sin, W_dq, W_uq, W_uk, W_qr
         regroup_x(2)
         quantise(nc, wqr_grouped[:], wqr_mx)
         make_keff(1, 2, nc.scalar.copy)
-        make_keff(1, 3, nc.vector.tensor_copy)
+        make_keff(1, 3, nc.scalar.copy)
         quantise_x(2)
         make_trig()
         quantise_keff(1)
@@ -301,7 +316,7 @@ def tile_causalselfattention_pa_t_kernel(tc, x, cos, sin, W_dq, W_uq, W_uk, W_qr
                 transpose_x(pair + 3)
                 regroup_x(pair + 3)
             if not last:
-                project_cq(pair + 1, on_vector)
+                project_cq(pair + 1, on_vector if pair + 3 < N_PAIRS else on_both)
             project_cqr(pair)
             rotate(pair)
             sum_q_r(pair)

@@ -84,13 +84,10 @@ def tile_causalselfattention_pa_t_kernel(tc, x, cos, sin, W_dq, W_uq, W_uk, W_qr
         wuq_view = W_uq.rearrange("(m j) c -> m j c", j=PACK)
         wdq_view = W_dq.rearrange("(m j) k -> m j k", j=PACK)
 
-        def load_halves(view, width, name):
-            halves = []
-            for half in range(2):
-                rows = const.tile([P, 2, width], BF16, name="%s_rows%d" % (name, half))
-                nc.sync.dma_start(out=rows[:], in_=view[:, 2 * half : 2 * half + 2, :])
-                halves.append(rows[:].bitcast(F32))
-            return [halves[j // 2][:, j % 2, :] for j in range(PACK)]
+        def load_half(view, half, width, name):
+            rows = const.tile([P, 2, width], BF16, name="%s_rows%d" % (name, half))
+            nc.sync.dma_start(out=rows[:], in_=view[:, 2 * half : 2 * half + 2, :])
+            return [rows[:, j, :].bitcast(F32) for j in range(2)]
 
         wuk_view = W_uk.rearrange("(h q e) n -> h q e n", h=NH, e=WORDS)
         wuk_rows = []
@@ -100,9 +97,10 @@ def tile_causalselfattention_pa_t_kernel(tc, x, cos, sin, W_dq, W_uq, W_uk, W_qr
             nc.sync.dma_start(out=rows[:], in_=wuk_view[h])
             wuk_rows.append(rows)
 
-        wuq_words = load_halves(wuq_view, NH * HS, "wuq")
+        wuq_words = [words for half in range(2) for words in load_half(wuq_view, half, NH * HS, "wuq")]
+        wdq_words = load_half(wdq_view, 0, C, "wdq")
         load_wuk(0)
-        wdq_words = load_halves(wdq_view, C, "wdq")
+        wdq_words += load_half(wdq_view, 1, C, "wdq")
         load_x(0, 0, PAIR)
         load_x(0, PAIR, PAIR)
         load_wuk(1)
@@ -141,18 +139,21 @@ def tile_causalselfattention_pa_t_kernel(tc, x, cos, sin, W_dq, W_uq, W_uk, W_qr
             copy(out=grouped.bitcast(F32), in_=bank[:].rearrange("p u c -> p c u"))
 
         wuq_t = []
+        wuq_banks = [qa_banks.tile([P, PACK, P], F32, tag="bank", name="bank") for h in range(NH)]
+        for half in range(2):
+            for h in range(NH):
+                for j in (2 * half, 2 * half + 1):
+                    nc.tensor.transpose(wuq_banks[h][:, j, :], wuq_words[j][:, h * P : (h + 1) * P], identity[:])
         for h, copy in enumerate((nc.scalar.copy, nc.vector.tensor_copy)):
-            bank = qa_banks.tile([P, PACK, P], F32, tag="bank")
-            for j in range(PACK):
-                nc.tensor.transpose(bank[:, j, :], wuq_words[j][:, h * P : (h + 1) * P], identity[:])
             transposed = const.tile([P, PACK * P], F32, name="wuq_t%d" % h)
-            copy(out=transposed[:], in_=bank[:].rearrange("p j m -> p (j m)"))
+            copy(out=transposed[:], in_=wuq_banks[h][:].rearrange("p j m -> p (j m)"))
             wuq_t.append(transposed[:].bitcast(BF16).rearrange("p (c e) -> p c e", e=WORDS))
         warm_up(2)
 
         wdq_grouped = const.tile([P, NLQ, PACK], BF16, align_bytes=64)
         wdq_mx = mx_tiles(const, NLQ, "wdq")
-        for half, copy in enumerate((nc.scalar.copy, nc.vector.tensor_copy)):
+
+        def transpose_wdq(half, copy):
             bank = qa_banks.tile([P, WORDS, PAIR * P], F32, tag="bank")
             transpose_two_tiles(bank, wdq_words[PAIR * half : PAIR * (half + 1)])
             regroup_words(copy, wdq_grouped[:, PAIR * P * half : PAIR * P * (half + 1), :], bank)
@@ -206,8 +207,10 @@ def tile_causalselfattention_pa_t_kernel(tc, x, cos, sin, W_dq, W_uq, W_uk, W_qr
             first = h * NLKV + n_block * P
             copy(out=keff_grouped[:, first : first + P, :], in_=bank[:].rearrange("p j n -> p n j"))
 
-        def quantise_keff(h):
-            quantise(nc, keff_grouped[:, h * NLKV : (h + 1) * NLKV, :], columns(keff_mx, h * NLKV, NLKV))
+        def quantise_keff(h, half):
+            count = NLKV // 2
+            first = h * NLKV + half * count
+            quantise(nc, keff_grouped[:, first : first + count, :], columns(keff_mx, first, count))
 
         wqr_grouped = const.tile([P, ROT, PACK], BF16, align_bytes=64)
         wqr_mx = mx_tiles(const, ROT, "wqr")
@@ -284,7 +287,9 @@ def tile_causalselfattention_pa_t_kernel(tc, x, cos, sin, W_dq, W_uq, W_uk, W_qr
 
         on_vector = (nc.vector.tensor_copy, nc.vector.tensor_copy)
 
+        transpose_wdq(0, nc.scalar.copy)
         make_keff(0, 0, nc.scalar.copy)
+        transpose_wdq(1, nc.vector.tensor_copy)
         transpose_x(0)
         regroup_x(0)
         quantise(nc, wdq_grouped[:], wdq_mx)
@@ -299,16 +304,18 @@ def tile_causalselfattention_pa_t_kernel(tc, x, cos, sin, W_dq, W_uq, W_uk, W_qr
         quantise_x(1)
         transpose_wqr()
         make_keff(1, 0, nc.scalar.copy)
+        quantise_keff(0, 0)
         make_keff(1, 1, nc.vector.tensor_copy)
-        quantise_keff(0)
+        quantise_keff(0, 1)
         transpose_x(2)
         regroup_x(2)
         quantise(nc, wqr_grouped[:], wqr_mx)
         make_keff(1, 2, nc.scalar.copy)
         make_keff(1, 3, nc.scalar.copy)
         quantise_x(2)
+        quantise_keff(1, 0)
         make_trig()
-        quantise_keff(1)
+        quantise_keff(1, 1)
 
         for pair in range(N_PAIRS):
             last = pair == N_PAIRS - 1

@@ -121,7 +121,7 @@ def tile_causalselfattention_pa_t_kernel(tc, x, cos, sin, W_dq, W_uq, W_uk, W_qr
         make_identity(nc, identity[:])
 
         zeros = const.tile([P, NLKV], BF16)
-        nc.vector.memset(zeros[:], 0.0)
+        nc.vector.memset(zeros[:].bitcast(U32), 0)
 
         def warm_up(count):
             for i in range(count):
@@ -239,10 +239,10 @@ def tile_causalselfattention_pa_t_kernel(tc, x, cos, sin, W_dq, W_uq, W_uk, W_qr
         trig = const.tile([P, TILES_PER_BATCH, 2, 2, DHR // 2], BF16)
 
         def make_trig():
-            for e, f, table, factor in ((0, 0, 0, 1.0), (1, 1, 0, 1.0), (0, 1, 1, 1.0), (1, 0, 1, -1.0)):
-                nc.gpsimd.tensor_scalar(
-                    out=trig[:, :, e, f, :], in0=trig_rows[:, table, :, :], scalar1=factor, scalar2=0.0, op0=MULT, op1=ADD
-                )
+            for e in range(2):
+                nc.vector.tensor_copy(out=trig[:, :, e, e, :], in_=trig_rows[:, 0, :, :])
+            nc.vector.tensor_copy(out=trig[:, :, 0, 1, :], in_=trig_rows[:, 1, :, :])
+            nc.vector.tensor_scalar_mul(trig[:, :, 1, 0, :], trig_rows[:, 1, :, :], -1.0)
 
         def rotate(pair):
             a = pair * PAIR % TILES_PER_BATCH

from contextlib import ExitStack

import concourse.mybir as mybir
from concourse.masks import make_identity

F32 = mybir.dt.float32
BF16 = mybir.dt.bfloat16
U32 = mybir.dt.uint32
U8 = mybir.dt.uint8
FP8X4 = mybir.dt.float8_e4m3fn_x4
MULT = mybir.AluOpType.mult
ADD = mybir.AluOpType.add

B, T, C = 4, 1024, 512
NH, HS = 2, 256
NLQ, NLKV, DHR = 512, 512, 128

P = 128
PACK = 4
WORDS = 2
ROT = NH * DHR
TILES_PER_BATCH = T // P
PAIR = 2
GROUP = 4
N_PAIRS = B * TILES_PER_BATCH // PAIR
N_GROUPS = B * TILES_PER_BATCH // GROUP
GROUPS_PER_BATCH = TILES_PER_BATCH // GROUP

FLOPS = 2 * B * T * NLQ * (C + NH * NLKV + ROT) + 2 * NH * NLQ * HS * NLKV


def quantise(nc, grouped, operand):
    codes, scales = operand
    nc.vector.quantize_mx(
        out=codes.bitcast(FP8X4), scales=scales, in_=grouped.rearrange("p c t -> p (c t)")
    )


def columns(operand, first, count):
    codes, scales = operand
    return codes[:, first : first + count], scales[:, first : first + count]


def mx_pass(nc, out, stationary, moving):
    nc.tensor.matmul_mx(
        out=out,
        lhsT=stationary[0].bitcast(FP8X4),
        lhsT_scale=stationary[1],
        rhs=moving[0].bitcast(FP8X4),
        rhs_scale=moving[1],
        start=True,
        stop=True,
    )


def tile_causalselfattention_pa_t_kernel(tc, x, cos, sin, W_dq, W_uq, W_uk, W_qr, out_0, out_1):
    nc = tc.nc
    with ExitStack() as ctx:
        ctx.enter_context(tc.manual_schedule())
        const = ctx.enter_context(tc.tile_pool(name="const", bufs=1))
        grouped_pool = ctx.enter_context(tc.tile_pool(name="grouped", bufs=3))
        mx_pool = ctx.enter_context(tc.tile_pool(name="mx", bufs=5))
        rope_pool = ctx.enter_context(tc.tile_pool(name="rope", bufs=3))
        rows_pool = ctx.enter_context(tc.tile_pool(name="rows", bufs=8))
        tr_banks = ctx.enter_context(tc.psum_pool(name="tr_banks", bufs=1))
        cq_banks = ctx.enter_context(tc.psum_pool(name="cq_banks", bufs=2))
        qa_banks = ctx.enter_context(tc.psum_pool(name="qa_banks", bufs=4))
        qr_banks = ctx.enter_context(tc.psum_pool(name="qr_banks", bufs=1))

        def mx_tiles(pool, width, name):
            codes = pool.tile([P, width], U32, name=name + "_codes", tag=name + "_codes", align_bytes=64)
            scales = pool.tile([P, width], U8, name=name + "_scales", tag=name + "_scales", align_bytes=64)
            return codes[:], scales[:]

        x_view = x.rearrange("b (p a) k -> b p a k", a=TILES_PER_BATCH)
        x_words = []

        def load_x(b, first, count):
            x_rows = const.tile([P, count, C], BF16, name="x_rows%d" % len(x_words))
            nc.sync.dma_start(out=x_rows[:], in_=x_view[b, :, first : first + count, :])
            words = x_rows[:].bitcast(F32)
            x_words.extend(words[:, s, :] for s in range(count))

        wuq_view = W_uq.rearrange("(m j) c -> m j c", j=PACK)
        wdq_view = W_dq.rearrange("(m j) k -> m j k", j=PACK)

        def load_half(view, half, width, name):
            rows = const.tile([P, 2, width], BF16, name="%s_rows%d" % (name, half))
            nc.sync.dma_start(out=rows[:], in_=view[:, 2 * half : 2 * half + 2, :])
            return [rows[:, j, :].bitcast(F32) for j in range(2)]

        wuk_view = W_uk.rearrange("(h q e) n -> h q e n", h=NH, e=WORDS)
        wuk_rows = []

        def load_wuk(h):
            rows = const.tile([P, WORDS, NLKV], BF16, name="wuk_rows%d" % h)
            nc.sync.dma_start(out=rows[:], in_=wuk_view[h])
            wuk_rows.append(rows)

        wuq_words = [words for half in range(2) for words in load_half(wuq_view, half, NH * HS, "wuq")]
        wdq_words = load_half(wdq_view, 0, C, "wdq")
        load_wuk(0)
        wdq_words += load_half(wdq_view, 1, C, "wdq")
        load_x(0, 0, PAIR)
        load_x(0, PAIR, PAIR)
        load_wuk(1)
        wqr_rows = const.tile([P, 2, NLQ], BF16)
        nc.sync.dma_start(out=wqr_rows[:], in_=W_qr.rearrange("(m e) l -> m e l", e=2))
        def load_group(group):
            b, part = divmod(group, GROUPS_PER_BATCH)
            load_x(b, part * GROUP, GROUP)

        load_group(1)
        trig_rows = const.tile([P, 2, TILES_PER_BATCH, DHR // 2], BF16)
        for f, table in enumerate((cos, sin)):
            nc.sync.dma_start(out=trig_rows[:, f, :, :], in_=table.rearrange("(p a) i -> p a i", a=TILES_PER_BATCH))
        for group in range(2, N_GROUPS):
            load_group(group)

        identity = const.tile([P, P], F32)
        make_identity(nc, identity[:])

        zeros = const.tile([P, NLKV], BF16)
        nc.vector.memset(zeros[:].bitcast(U32), 0)

        def warm_up(count):
            for i in range(count):
                bank = cq_banks.tile([P, NLKV], F32, tag="bank", name="bank")
                nc.tensor.matmul(out=bank[:], lhsT=zeros[:, 0:P], rhs=zeros[:], start=True, stop=True)

        warm_up(5)

        def transpose_two_tiles(bank, tiles_of_words):
            for s, words in enumerate(tiles_of_words):
                for u in range(WORDS):
                    nc.tensor.transpose(bank[:, u, s * P : (s + 1) * P], words[:, u : WORDS * P : WORDS], identity[:])

        def regroup_words(copy, grouped, bank):
            copy(out=grouped.bitcast(F32), in_=bank[:].rearrange("p u c -> p c u"))

        wuq_t = []
        wuq_banks = [qa_banks.tile([P, PACK, P], F32, tag="bank", name="bank") for h in range(NH)]
        for half in range(2):
            for h in range(NH):
                for j in (2 * half, 2 * half + 1):
                    nc.tensor.transpose(wuq_banks[h][:, j, :], wuq_words[j][:, h * P : (h + 1) * P], identity[:])
        for h, copy in enumerate((nc.scalar.copy, nc.vector.tensor_copy)):
            transposed = const.tile([P, PACK * P], F32, name="wuq_t%d" % h)
            copy(out=transposed[:], in_=wuq_banks[h][:].rearrange("p j m -> p (j m)"))
            wuq_t.append(transposed[:].bitcast(BF16).rearrange("p (c e) -> p c e", e=WORDS))
        warm_up(2)

        wdq_grouped = const.tile([P, NLQ, PACK], BF16, align_bytes=64)
        wdq_mx = mx_tiles(const, NLQ, "wdq")

        def transpose_wdq(half, copy):
            bank = qa_banks.tile([P, WORDS, PAIR * P], F32, tag="bank")
            transpose_two_tiles(bank, wdq_words[PAIR * half : PAIR * (half + 1)])
            regroup_words(copy, wdq_grouped[:, PAIR * P * half : PAIR * P * (half + 1), :], bank)

        x_mx = {}
        cq_mx = {}
        x_grouped = {}
        cq_grouped = {}

        x_banks = {}

        def transpose_x(pair):
            x_banks[pair] = tr_banks.tile([P, WORDS, PAIR * P], F32, tag="bank", name="bank")
            transpose_two_tiles(x_banks[pair], x_words[pair * PAIR : (pair + 1) * PAIR])

        def regroup_x(pair):
            x_grouped[pair] = grouped_pool.tile([P, PAIR * P, PACK], BF16, tag="x", name="x", align_bytes=64)
            regroup_words(nc.scalar.copy, x_grouped[pair][:], x_banks[pair])

        def quantise_x(pair):
            x_mx[pair] = mx_tiles(mx_pool, PAIR * P, "x")
            quantise(nc, x_grouped[pair][:], x_mx[pair])

        def project_cq(pair, copies):
            grouped = grouped_pool.tile([P, PAIR * P, PACK], BF16, tag="cq", align_bytes=64)
            for s in range(PAIR):
                bank = cq_banks.tile([P, PACK, P], F32, tag="bank")
                for j in range(PACK):
                    mx_pass(nc, bank[:, j, :], columns(wdq_mx, j * P, P), columns(x_mx[pair], s * P, P))
                copies[s](out=grouped[:, s * P : (s + 1) * P, :], in_=bank[:].rearrange("p j t -> p t j"))
            cq_grouped[pair] = grouped

        def quantise_cq(pair):
            cq_mx[pair] = mx_tiles(mx_pool, PAIR * P, "cq")
            quantise(nc, cq_grouped[pair][:], cq_mx[pair])

        keff_grouped = const.tile([P, NH * NLKV, PACK], BF16, align_bytes=64)
        keff_mx = mx_tiles(const, NH * NLKV, "keff")

        def make_keff(h, n_block, copy):
            bank = qa_banks.tile([P, PACK, P], F32, tag="bank")
            for j in range(PACK):
                for e in range(WORDS):
                    nc.tensor.matmul(
                        out=bank[:, j, :],
                        lhsT=wuq_t[h][:, j * P : (j + 1) * P, e],
                        rhs=wuk_rows[h][:, e, n_block * P : (n_block + 1) * P],
                        start=(e == 0),
                        stop=(e == WORDS - 1),
                    )
            first = h * NLKV + n_block * P
            copy(out=keff_grouped[:, first : first + P, :], in_=bank[:].rearrange("p j n -> p n j"))

        def quantise_keff(h, half):
            count = NLKV // 2
            first = h * NLKV + half * count
            quantise(nc, keff_grouped[:, first : first + count, :], columns(keff_mx, first, count))

        wqr_grouped = const.tile([P, ROT, PACK], BF16, align_bytes=64)
        wqr_mx = mx_tiles(const, ROT, "wqr")

        def transpose_wqr():
            wqr_words = wqr_rows[:].bitcast(F32).rearrange("m e (p u) -> m e u p", u=WORDS)
            bank = qr_banks.tile([P, WORDS, ROT], F32, tag="bank")
            for e in range(2):
                for u in range(WORDS):
                    nc.tensor.transpose(bank[:, u, e * P : (e + 1) * P], wqr_words[:, e, u, :], identity[:])
            regroup_words(nc.scalar.copy, wqr_grouped[:], bank)

        q_abs_view = out_0.rearrange("b h (p a) n -> b h p a n", a=TILES_PER_BATCH)
        q_r_view = out_1.rearrange("b (p a) h d -> b p a (h d)", a=TILES_PER_BATCH)
        rot_banks = {}
        products = {}
        q_r = {}

        def project_cqr(pair):
            rot_bank = qr_banks.tile([P, PAIR, 2 * P], F32, tag="bank")
            for s in range(PAIR):
                mx_pass(nc, rot_bank[:, s, :], columns(cq_mx[pair], s * P, P), wqr_mx)
            rot_banks[pair] = rot_bank
            products[pair] = rope_pool.tile([P, PAIR, 2, P, 2], F32, tag="products", name="products")

        trig = const.tile([P, TILES_PER_BATCH, 2, 2, DHR // 2], BF16)

        def make_trig():
            for e in range(2):
                nc.vector.tensor_copy(out=trig[:, :, e, e, :], in_=trig_rows[:, 0, :, :])
            nc.vector.tensor_copy(out=trig[:, :, 0, 1, :], in_=trig_rows[:, 1, :, :])
            nc.vector.tensor_scalar_mul(trig[:, :, 1, 0, :], trig_rows[:, 1, :, :], -1.0)

        def rotate(pair):
            a = pair * PAIR % TILES_PER_BATCH
            half = DHR // 2
            for h in range(NH):
                heads = slice(h * half, (h + 1) * half)
                nc.vector.tensor_tensor(
                    out=products[pair][:, :, :, heads, :].rearrange("p s e i f -> p (s e) i f"),
                    in0=rot_banks[pair][:].rearrange("p s (e m) -> p (s e) m", e=2)[:, :, heads]
                    .unsqueeze(3)
                    .to_broadcast([P, PAIR * 2, half, 2]),
                    in1=trig[:, a : a + PAIR, :, :, :].rearrange("p s e f i -> p (s e) i f"),
                    op=MULT,
                )

        def sum_q_r(pair):
            b, a = divmod(pair * PAIR, TILES_PER_BATCH)
            q_r_rows = rows_pool.tile([P, PAIR, ROT], F32, tag="q_r")
            nc.gpsimd.tensor_tensor(
                out=q_r_rows[:],
                in0=products[pair][:, :, 0, :, :].rearrange("p s m f -> p s (m f)"),
                in1=products[pair][:, :, 1, :, :].rearrange("p s m f -> p s (m f)"),
                op=ADD,
            )
            q_r[pair] = q_r_rows

        def store_q_r(pair):
            b, a = divmod(pair * PAIR, TILES_PER_BATCH)
            nc.sync.dma_start(out=q_r_view[b, :, a : a + PAIR, :], in_=q_r[pair][:])

        def project_q_abs(pair, h, copies):
            b, a = divmod(pair * PAIR, TILES_PER_BATCH)
            q_abs_rows = rows_pool.tile([P, PAIR, NLKV], F32, tag="q_abs")
            for s in range(PAIR):
                acc = qa_banks.tile([P, NLKV], F32, tag="bank")
                mx_pass(nc, acc[:], columns(cq_mx[pair], s * P, P), columns(keff_mx, h * NLKV, NLKV))
                copies[s](out=q_abs_rows[:, s, :], in_=acc[:])
            nc.sync.dma_start(out=q_abs_view[b, h, :, a : a + PAIR, :], in_=q_abs_rows[:])

        on_scalar = (nc.scalar.copy, nc.scalar.copy)
        on_both = (nc.scalar.copy, nc.vector.tensor_copy)

        on_vector = (nc.vector.tensor_copy, nc.vector.tensor_copy)

        transpose_wdq(0, nc.scalar.copy)
        make_keff(0, 0, nc.scalar.copy)
        transpose_wdq(1, nc.vector.tensor_copy)
        transpose_x(0)
        regroup_x(0)
        quantise(nc, wdq_grouped[:], wdq_mx)
        quantise_x(0)
        make_keff(0, 1, nc.vector.tensor_copy)
        make_keff(0, 2, nc.scalar.copy)
        make_keff(0, 3, nc.vector.tensor_copy)
        project_cq(0, (nc.vector.tensor_copy, nc.scalar.copy))
        transpose_x(1)
        regroup_x(1)
        quantise_cq(0)
        quantise_x(1)
        transpose_wqr()
        make_keff(1, 0, nc.scalar.copy)
        quantise_keff(0, 0)
        make_keff(1, 1, nc.vector.tensor_copy)
        quantise_keff(0, 1)
        transpose_x(2)
        regroup_x(2)
        quantise(nc, wqr_grouped[:], wqr_mx)
        make_keff(1, 2, nc.scalar.copy)
        make_keff(1, 3, nc.scalar.copy)
        quantise_x(2)
        quantise_keff(1, 0)
        make_trig()
        quantise_keff(1, 1)

        for pair in range(N_PAIRS):
            last = pair == N_PAIRS - 1
            if pair + 3 < N_PAIRS:
                transpose_x(pair + 3)
                regroup_x(pair + 3)
            if not last:
                project_cq(pair + 1, on_vector if pair + 3 < N_PAIRS else on_both)
            project_cqr(pair)
            rotate(pair)
            sum_q_r(pair)
            if not last:
                quantise_cq(pair + 1)
            if pair + 3 < N_PAIRS:
                quantise_x(pair + 3)
            for h in range(NH):
                project_q_abs(pair, h, on_both if last else on_scalar)
            store_q_r(pair)
